import numpy as np
import ml_dtypes


def mxq(x, axis, fmt="e4m3"):
    dtype, down = {"e4m3": (ml_dtypes.float8_e4m3fn, 7), "e5m2": (ml_dtypes.float8_e5m2, 14)}[fmt]
    v = np.moveaxis(np.asarray(x, np.float32).astype(ml_dtypes.bfloat16).astype(np.float64), axis, -1)
    blocks = v.reshape(v.shape[:-1] + (-1, 32))
    amax = np.abs(blocks).max(-1, keepdims=True)
    byte = np.maximum(np.where(amax > 0, np.frexp(amax)[1] - 1 + 127, 0) - down, 1)
    scale = np.exp2(byte - 127.0)
    codes = (blocks / scale).astype(np.float32).astype(dtype).astype(np.float64)
    return np.moveaxis((codes * scale).reshape(v.shape), -1, axis)


WIDE = False


def mx_kscale(k):
    if not WIDE:
        return np.ones(k)
    levels = np.array([10, -10, 5, -5, 0])
    if k % 512:
        return np.exp2(np.random.permutation(np.resize(levels, k // 32))).repeat(32)
    a = np.empty((k // 512, 16))
    for p in range(k // 512):
        a[p, :8] = np.random.permutation(np.resize(levels, 8))
        for g in range(8):
            far = levels[np.abs(levels - a[p, g]) >= 10]
            a[p, g + 8] = far[np.random.randint(len(far))]
    return np.exp2(a.ravel()).repeat(32)


BF16 = ml_dtypes.bfloat16


def bf(x):
    return np.asarray(x, np.float32).astype(BF16)


def f64(x):
    return np.asarray(x).astype(np.float64)


B, S, D, H, C = 1, 1024, 1024, 1024, 512


def draw0():
    s, t = mx_kscale(H), mx_kscale(S)
    return {"q": bf(np.random.standard_normal((B, S, H)) * 0.6 * s),
            "k": bf(np.random.standard_normal((B, S, H)) * 0.6 / s * t[:, None]),
            "v": bf(np.random.standard_normal((B, S, H)) * 0.6 / t[:, None]),
            "decay": bf(np.random.uniform(0.5, 1.5, S) * 2.0 / S)}


def core(q, k, v, decay):
    qq = mxq(f64(q), 2, "e4m3")
    kq = mxq(f64(k), 2, "e4m3")
    vq = mxq(f64(v), 1, "e4m3")
    idx = np.arange(S)
    diff = f64(np.abs(idx[None, :] - idx[:, None]))
    dm = np.exp(-f64(decay)[None, :] * diff) * np.tril(np.ones((S, S)))
    out = np.zeros((B, S, H))
    for r in range(0, S, C):
        e = r + C
        sc = (qq[:, r:e] @ kq[:, :e].transpose(0, 2, 1)) * dm[r:e, :e]
        sc = sc / np.sqrt(H)
        out[:, r:e] = mxq(sc, 2, "e4m3") @ vq[:, :e]
    return out


def e4m3fn_bytes(y):
    return np.clip(np.asarray(y, np.float64), -448.0, 448.0).astype(np.float32).astype(ml_dtypes.float8_e4m3fn).view(np.uint8)


def e4m3fn_values(b):
    return np.asarray(b, np.uint8).view(ml_dtypes.float8_e4m3fn).astype(np.float64)


def setup_inputs():
    d = draw0()
    x0 = np.asarray(d['v']).astype(np.float64)
    s = (np.max(np.abs(x0), axis=(0, 2), keepdims=True) / 448.0).astype(np.float32)
    out = {}
    for k, v in d.items():
        if k == 'v':
            out['v_bytes'] = e4m3fn_bytes(x0 / s.astype(np.float64))
            out['v_scale'] = s
        else:
            out[k] = v
    return out


def reference(q, k, v_bytes, v_scale, decay):
    return core(q, k, e4m3fn_values(v_bytes) * v_scale.astype(np.float64), decay)

@@ -1,0 +1,348 @@
+from contextlib import ExitStack
+
+import concourse.mybir as mybir
+from concourse.masks import make_identity
+
+F32 = mybir.dt.float32
+BF16 = mybir.dt.bfloat16
+U32 = mybir.dt.uint32
+U8 = mybir.dt.uint8
+E4M3FN = mybir.dt.float8_e4m3fn
+FP8X4 = mybir.dt.float8_e4m3fn_x4
+ALU = mybir.AluOpType
+ACT = mybir.ActivationFunctionType
+
+FLOPS = 2 * 1024 * (512 * 512 + 512 * 1024) * 2
+BIG = 2.0**100
+
+
+def tile_simplifiedretnet_pa_kernel(tc, q, k, v_bytes, v_scale, decay, out):
+    nc = tc.nc
+    x_rows = {
+        "q": q.rearrange("o (c m b) f -> (o c) m b f", c=2, b=4),
+        "k": k.rearrange("o (c m b) f -> (o c) m b f", c=2, b=4),
+    }
+    v_rows = v_bytes.rearrange("o (g p t) n -> (o g) p t n", g=2, t=4)
+    o_rows = out.rearrange("o (c m b) n -> (o c) m b n", c=2, b=4)
+
+    with ExitStack() as ctx:
+        keep = ctx.enter_context(tc.tile_pool(name="keep", bufs=1))
+        ps_tp = ctx.enter_context(tc.psum_pool(name="ps_tp", bufs=3))
+        ps_sc = ctx.enter_context(tc.psum_pool(name="ps_sc", bufs=2))
+        ps_po = ctx.enter_context(tc.psum_pool(name="ps_po", bufs=3))
+        ctx.enter_context(tc.manual_schedule())
+
+        def sb(name, shape, dtype):
+            return keep.tile(shape, dtype, name=name, align_bytes=64)
+
+        raw = {(x, c): sb("raw_%s_%s" % (x, c,), [128, 4, 1024], BF16) for x in "qk" for c in range(2)}
+        grouped = {(x, c, b): sb("grp_%s_%s_%s" % (x, c, b,), [128, 2, 128, 2], F32) for x in "qk" for c in range(2) for b in range(4)}
+        codes = {(x, c, b): sb("cod_%s_%s_%s" % (x, c, b,), [128, 256], U32) for x in "qk" for c in range(2) for b in range(4)}
+        scales = {(x, c, b): sb("scl_%s_%s_%s" % (x, c, b,), [128, 256], U8) for x in "qk" for c in range(2) for b in range(4)}
+        vb = [sb("vb%s" % (g,), [128, 4, 1024], U8) for g in range(2)]
+        wide = [sb("wide%s" % (g,), [128, 4, 1024], BF16) for g in range(2)]
+        vi = {(g, h): sb("vi%s_%s" % (g, h,), [128, 512, 4], BF16) for g in range(2) for h in range(2)}
+        v_codes = {(g, h): sb("vc%s_%s" % (g, h,), [128, 512], U32) for g in range(2) for h in range(2)}
+        v_scl = {(g, h): sb("vx%s_%s" % (g, h,), [128, 512], U8) for g in range(2) for h in range(2)}
+        gain = [sb("gain%s" % (e,), [128, 4, 512], F32) for e in range(3)]
+        pairs = [(0, 0), (0, 1), (1, 1)]
+        s_bf = {(g, c, b): sb("s%s_%s_%s" % (g, c, b,), [128, 128, 4], BF16) for g, c in pairs for b in range(4)}
+        s_codes = {(g, c, b): sb("sc%s_%s_%s" % (g, c, b,), [128, 128], U32) for g, c in pairs for b in range(4)}
+        s_scl = {(g, c, b): sb("sx%s_%s_%s" % (g, c, b,), [128, 128], U8) for g, c in pairs for b in range(4)}
+        result = {(c, b, h): sb("o%s_%s_%s" % (c, b, h,), [128, 512], F32) for c in range(2) for b in range(4) for h in range(2)}
+        ident = sb("ident", [128, 128], F32)
+        dist = sb("dist", [128, 7, 128], F32)
+        near = sb("near", [128, 7, 128], F32)
+        far = sb("far", [128, 7, 128], F32)
+        dk = sb("dk", [128, 2, 4], BF16)
+        nd = sb("nd", [128, 8], F32)
+        vs = sb("vs", [128, 2, 4], F32)
+        warm = sb("warm", [128, 8], F32)
+        warm_out = sb("warm_out", [128, 8], F32)
+        zeros = sb("zeros", [128, 512], BF16)
+
+        psum = {}
+
+        def load(name, c, lo, hi):
+            if name == "v":
+                nc.sync.dma_start(out=vb[c][:, lo:hi, :], in_=v_rows[c][:, lo:hi, :])
+            else:
+                nc.sync.dma_start(out=raw[name, c][:, lo:hi, :], in_=x_rows[name][c][:, lo:hi, :])
+
+        def TR(x, c, b):
+            bank = ps_tp.tile([128, 2, 2, 128], F32, name="tp")
+            psum[x, c, b] = bank
+            words = raw[x, c][:, b, :].bitcast(F32)
+            for g in range(2):
+                for u in range(2):
+                    nc.tensor.transpose(bank[:, g, u, :], words[:, 256 * g + u : 256 * (g + 1) : 2], ident[:])
+
+        def CP(x, c, b, eng="S"):
+            src = psum[x, c, b][:].rearrange("p g u r -> p g r u")
+            if eng == "S":
+                nc.scalar.copy(grouped[x, c, b][:], src)
+            else:
+                nc.vector.tensor_copy(out=grouped[x, c, b][:], in_=src)
+
+        def QZ(x, c, b):
+            nc.vector.quantize_mx(
+                out=codes[x, c, b][:].bitcast(FP8X4),
+                scales=scales[x, c, b][:],
+                in_=grouped[x, c, b][:].rearrange("p g r u -> p (g r u)").bitcast(BF16),
+            )
+
+        def WD(g, t, eng="V"):
+            src = vb[g][:, t, :].bitcast(E4M3FN)
+            if eng == "V":
+                nc.vector.tensor_scalar(out=wide[g][:, t, :], in0=src, scalar1=vs[:, g, t : t + 1], scalar2=None, op0=ALU.mult)
+            else:
+                nc.scalar.activation(out=wide[g][:, t, :], in_=src, func=ACT.Copy, scale=vs[:, g, t : t + 1])
+
+        def IL(g, h):
+            nc.vector.tensor_copy(out=vi[g, h][:], in_=wide[g][:, :, 512 * h : 512 * (h + 1)].rearrange("p t n -> p n t"))
+
+        def QV(g, h):
+            nc.vector.quantize_mx(
+                out=v_codes[g, h][:].bitcast(FP8X4), scales=v_scl[g, h][:], in_=vi[g, h][:].rearrange("p n t -> p (n t)")
+            )
+
+        def EX(e, t):
+            table = far if e == 1 else near
+            col = 4 * (e // 2) + t
+            nc.scalar.activation(
+                out=gain[e][:, t, :],
+                in_=table[:, 3 - t : 7 - t, :].rearrange("p b m -> p (b m)"),
+                func=ACT.Exp,
+                scale=nd[:, col : col + 1],
+            )
+
+        def M1(g, c, b, pool="sc"):
+            bank = (ps_sc if pool == "sc" else ps_tp).tile([128, 4, 128], F32, name=pool)
+            psum["s", g, c, b] = bank
+            for t in range(4):
+                for f in range(2):
+                    cols = slice(128 * f, 128 * (f + 1))
+                    nc.tensor.matmul_mx(
+                        out=bank[:, t, :],
+                        lhsT=codes["k", g, t][:, cols].bitcast(FP8X4),
+                        lhsT_scale=scales["k", g, t][:, cols],
+                        rhs=codes["q", c, b][:, cols].bitcast(FP8X4),
+                        rhs_scale=scales["q", c, b][:, cols],
+                        start=(f == 0),
+                        stop=(f == 1),
+                    )
+
+        def MK(g, c, b):
+            nc.vector.scalar_tensor_tensor(
+                out=s_bf[g, c, b][:],
+                in0=psum["s", g, c, b][:].rearrange("p t i -> p i t"),
+                scalar=1.0 / 32.0,
+                in1=gain[g + c][:, :, 128 * b : 128 * (b + 1)].rearrange("p t i -> p i t"),
+                op0=ALU.mult,
+                op1=ALU.mult,
+            )
+
+        def QS(g, c, b):
+            nc.vector.quantize_mx(
+                out=s_codes[g, c, b][:].bitcast(FP8X4),
+                scales=s_scl[g, c, b][:],
+                in_=s_bf[g, c, b][:].rearrange("p i t -> p (i t)"),
+            )
+
+        def M2(c, b, h, gs=None, pool="po"):
+            if gs is None:
+                gs = range(c + 1)
+            if ("o", c, b, h) not in psum:
+                psum["o", c, b, h] = (ps_po if pool == "po" else ps_tp).tile([128, 512], F32, name=pool)
+            for g in gs:
+                nc.tensor.matmul_mx(
+                    out=psum["o", c, b, h][:],
+                    lhsT=s_codes[g, c, b][:].bitcast(FP8X4),
+                    lhsT_scale=s_scl[g, c, b][:],
+                    rhs=v_codes[g, h][:].bitcast(FP8X4),
+                    rhs_scale=v_scl[g, h][:],
+                    start=(g == 0),
+                    stop=(g == c),
+                )
+
+        def CO(c, b, h, eng="S"):
+            src = psum["o", c, b, h]
+            res = result[c, b, h]
+            if eng == "S":
+                nc.scalar.copy(res[:], src[:])
+            else:
+                nc.vector.tensor_copy(out=res[:], in_=src[:])
+            nc.sync.dma_start(out=o_rows[c][:, b, 512 * h : 512 * (h + 1)], in_=res[:])
+
+        def DUMMY(n, width=512):
+            bank = ps_sc.tile([128, 512], F32, name="sc")
+            for i in range(n):
+                nc.tensor.matmul(bank[:, :width], lhsT=zeros[:, :128], rhs=zeros[:, :width], start=True, stop=True)
+
+        nc.scalar.dma_start(out=dk[:], in_=decay.rearrange("(g p t) -> p g t", g=2, t=4))
+        nc.scalar.dma_start(out=vs[:], in_=v_scale.rearrange("o (g p t) i -> p (o g) (t i)", g=2, t=4))
+        load("v", 0, 0, 2)
+        load("v", 0, 2, 4)
+        for x, c in (("k", 0), ("q", 0), ("q", 1), ("k", 1)):
+            load(x, c, 0, 2)
+            load(x, c, 2, 4)
+        load("v", 1, 0, 4)
+        nc.vector.memset(warm[:], 0.0)
+        nc.vector.memset(zeros[:], 0.0)
+        nc.scalar.activation(out=warm_out[:], in_=warm[:], func=ACT.Exp)
+        nc.gpsimd.iota(dist[:], pattern=[[1, 7], [4, 128]], base=-3, channel_multiplier=-4, allow_small_or_imprecise_dtypes=True)
+        make_identity(nc, ident[:])
+        nc.gpsimd.iota(far[:], pattern=[[1, 7], [4, 128]], base=509, channel_multiplier=-4, allow_small_or_imprecise_dtypes=True)
+        nc.vector.scalar_tensor_tensor(out=near[:], in0=dist[:], scalar=-BIG, in1=dist[:], op0=ALU.mult, op1=ALU.max)
+        nc.vector.tensor_scalar(out=nd[:], in0=dk[:].rearrange("p g t -> p (g t)"), scalar1=1.0 / 2.0**90, scalar2=-1.0, op0=ALU.max, op1=ALU.mult)
+
+        DUMMY(6)
+        EX(0, 0)
+        EX(0, 1)
+        EX(0, 2)
+        EX(0, 3)
+        WD(0, 0, 'V')
+        WD(0, 1, 'V')
+        WD(0, 2, 'V')
+        WD(0, 3, 'V')
+        TR('k', 0, 0)
+        CP('k', 0, 0)
+        TR('k', 0, 1)
+        CP('k', 0, 1)
+        DUMMY(1)
+        TR('k', 0, 2)
+        CP('k', 0, 2)
+        TR('k', 0, 3)
+        CP('k', 0, 3)
+        DUMMY(1)
+        IL(0, 0)
+        QZ('k', 0, 0)
+        QZ('k', 0, 1)
+        QZ('k', 0, 2)
+        QZ('k', 0, 3)
+        TR('q', 0, 0)
+        CP('q', 0, 0)
+        TR('q', 0, 1)
+        CP('q', 0, 1)
+        DUMMY(1)
+        TR('q', 0, 2)
+        CP('q', 0, 2)
+        TR('q', 0, 3)
+        CP('q', 0, 3)
+        QZ('q', 0, 0)
+        QZ('q', 0, 1)
+        M1(0, 0, 0)
+        M1(0, 0, 1)
+        IL(0, 1)
+        EX(1, 0)
+        EX(1, 1)
+        TR('q', 1, 0)
+        CP('q', 1, 0)
+        TR('q', 1, 1)
+        CP('q', 1, 1)
+        TR('q', 1, 2)
+        CP('q', 1, 2)
+        QZ('q', 0, 2)
+        MK(0, 0, 0)
+        QZ('q', 0, 3)
+        MK(0, 0, 1)
+        QV(0, 0)
+        QS(0, 0, 0)
+        M1(0, 0, 2)
+        M1(0, 0, 3)
+        EX(1, 2)
+        EX(1, 3)
+        TR('q', 1, 3)
+        CP('q', 1, 3)
+        QZ('q', 1, 0)
+        QV(0, 1)
+        MK(0, 0, 2)
+        QS(0, 0, 1)
+        QZ('q', 1, 1)
+        MK(0, 0, 3)
+        QS(0, 0, 2)
+        QZ('q', 1, 2)
+        TR('k', 1, 0)
+        CP('k', 1, 0)
+        TR('k', 1, 1)
+        CP('k', 1, 1)
+        TR('k', 1, 2)
+        CP('k', 1, 2)
+        QZ('q', 1, 3)
+        QS(0, 0, 3)
+        M1(0, 1, 0)
+        M1(0, 1, 1)
+        WD(1, 0, 'V')
+        WD(1, 1, 'V')
+        WD(1, 2, 'V')
+        TR('k', 1, 3)
+        CP('k', 1, 3)
+        M2(0, 0, 0)
+        M2(0, 1, 0)
+        M2(0, 2, 0)
+        WD(1, 3, 'S')
+        QZ('k', 1, 0)
+        MK(0, 1, 0)
+        QZ('k', 1, 1)
+        CO(0, 0, 0)
+        CO(0, 1, 0)
+        CO(0, 2, 0)
+        QZ('k', 1, 2)
+        QS(0, 1, 0)
+        MK(0, 1, 1)
+        QZ('k', 1, 3)
+        M1(0, 1, 2)
+        M1(1, 1, 0, 'tp')
+        M1(1, 1, 1, 'tp')
+        QS(0, 1, 1)
+        IL(1, 0)
+        IL(1, 1)
+        EX(2, 0)
+        EX(2, 1)
+        EX(2, 2)
+        EX(2, 3)
+        M2(0, 3, 0)
+        M2(0, 0, 1)
+        M2(0, 1, 1)
+        CO(0, 3, 0)
+        CO(0, 0, 1)
+        CO(0, 1, 1)
+        M1(0, 1, 3)
+        M1(1, 1, 2, 'tp')
+        M2(0, 2, 1)
+        M2(0, 3, 1)
+        CO(0, 2, 1)
+        CO(0, 3, 1)
+        QV(1, 0)
+        MK(1, 1, 0)
+        QV(1, 1)
+        QS(1, 1, 0)
+        M1(1, 1, 3, 'tp')
+        MK(1, 1, 1)
+        MK(0, 1, 2)
+        M2(1, 0, 0)
+        CO(1, 0, 0)
+        M2(1, 0, 1)
+        CO(1, 0, 1)
+        QS(1, 1, 1)
+        MK(1, 1, 2)
+        QS(0, 1, 2)
+        M2(1, 1, 0)
+        CO(1, 1, 0)
+        M2(1, 1, 1)
+        CO(1, 1, 1)
+        MK(0, 1, 3)
+        QS(1, 1, 2)
+        M2(1, 2, 0)
+        CO(1, 2, 0)
+        M2(1, 2, 1)
+        CO(1, 2, 1)
+        MK(1, 1, 3)
+        QS(0, 1, 3)
+        QS(1, 1, 3)
+        M2(1, 3, 0, (0,))
+        M2(1, 3, 1, (0,))
+        M2(1, 3, 0, (1,))
+        CO(1, 3, 0)
+        M2(1, 3, 1, (1,))
+        CO(1, 3, 1, 'V')

@@ -1,3 +1,4 @@
+import math
 from contextlib import ExitStack
 
 import concourse.mybir as mybir
@@ -14,6 +15,7 @@ ACT = mybir.ActivationFunctionType
 
 FLOPS = 2 * 1024 * (512 * 512 + 512 * 1024) * 2
 BIG = 2.0**100
+LOG_SCALE = -5.0 * math.log(2.0)
 
 
 def tile_simplifiedretnet_pa_kernel(tc, q, k, v_bytes, v_scale, decay, out):
@@ -44,7 +46,7 @@ def tile_simplifiedretnet_pa_kernel(tc, q, k, v_bytes, v_scale, decay, out):
         vi = {(g, h): sb("vi%s_%s" % (g, h,), [128, 512, 4], BF16) for g in range(2) for h in range(2)}
         v_codes = {(g, h): sb("vc%s_%s" % (g, h,), [128, 512], U32) for g in range(2) for h in range(2)}
         v_scl = {(g, h): sb("vx%s_%s" % (g, h,), [128, 512], U8) for g in range(2) for h in range(2)}
-        gain = [sb("gain%s" % (e,), [128, 4, 512], F32) for e in range(3)]
+        gain = [sb("gain%s" % (e,), [128, 128, 16], F32) for e in range(3)]
         pairs = [(0, 0), (0, 1), (1, 1)]
         s_bf = {(g, c, b): sb("s%s_%s_%s" % (g, c, b,), [128, 128, 4], BF16) for g, c in pairs for b in range(4)}
         s_codes = {(g, c, b): sb("sc%s_%s_%s" % (g, c, b,), [128, 128], U32) for g, c in pairs for b in range(4)}
@@ -53,7 +55,7 @@ def tile_simplifiedretnet_pa_kernel(tc, q, k, v_bytes, v_scale, decay, out):
         ident = sb("ident", [128, 128], F32)
         dist = sb("dist", [128, 7, 128], F32)
         near = sb("near", [128, 7, 128], F32)
-        far = sb("far", [128, 7, 128], F32)
+        far_bias = sb("far_bias", [128, 4], F32)
         dk = sb("dk", [128, 2, 4], BF16)
         nd = sb("nd", [128, 8], F32)
         vs = sb("vs", [128, 2, 4], F32)
@@ -99,7 +101,10 @@ def tile_simplifiedretnet_pa_kernel(tc, q, k, v_bytes, v_scale, decay, out):
                 nc.scalar.activation(out=wide[g][:, t, :], in_=src, func=ACT.Copy, scale=vs[:, g, t : t + 1])
 
         def IL(g, h):
-            nc.vector.tensor_copy(out=vi[g, h][:], in_=wide[g][:, :, 512 * h : 512 * (h + 1)].rearrange("p t n -> p n t"))
+            nc.vector.tensor_copy(
+                out=vi[g, h][:].rearrange("p (m i) t -> p m t i", i=4),
+                in_=wide[g][:, :, 512 * h : 512 * (h + 1)].rearrange("p t (m i) -> p m t i", i=4),
+            )
 
         def QV(g, h):
             nc.vector.quantize_mx(
@@ -107,12 +112,13 @@ def tile_simplifiedretnet_pa_kernel(tc, q, k, v_bytes, v_scale, decay, out):
             )
 
         def EX(e, t):
-            table = far if e == 1 else near
+            table = dist if e == 1 else near
             col = 4 * (e // 2) + t
             nc.scalar.activation(
-                out=gain[e][:, t, :],
-                in_=table[:, 3 - t : 7 - t, :].rearrange("p b m -> p (b m)"),
+                out=gain[e][:, :, 4 * t : 4 * (t + 1)],
+                in_=table[:, 3 - t : 7 - t, :].rearrange("p b (m i) -> p (b m) i", i=4),
                 func=ACT.Exp,
+                bias=far_bias[:, t : t + 1] if e == 1 else LOG_SCALE,
                 scale=nd[:, col : col + 1],
             )
 
@@ -133,13 +139,11 @@ def tile_simplifiedretnet_pa_kernel(tc, q, k, v_bytes, v_scale, decay, out):
                     )
 
         def MK(g, c, b):
-            nc.vector.scalar_tensor_tensor(
-                out=s_bf[g, c, b][:],
-                in0=psum["s", g, c, b][:].rearrange("p t i -> p i t"),
-                scalar=1.0 / 32.0,
-                in1=gain[g + c][:, :, 128 * b : 128 * (b + 1)].rearrange("p t i -> p i t"),
-                op0=ALU.mult,
-                op1=ALU.mult,
+            nc.vector.tensor_tensor(
+                out=s_bf[g, c, b][:].rearrange("p (m i) t -> p m t i", i=4),
+                in0=psum["s", g, c, b][:].rearrange("p t (m i) -> p m t i", i=4),
+                in1=gain[g + c][:, 32 * b : 32 * (b + 1), :].rearrange("p m (t i) -> p m t i", i=4),
+                op=ALU.mult,
             )
 
         def QS(g, c, b):
@@ -192,9 +196,9 @@ def tile_simplifiedretnet_pa_kernel(tc, q, k, v_bytes, v_scale, decay, out):
         nc.scalar.activation(out=warm_out[:], in_=warm[:], func=ACT.Exp)
         nc.gpsimd.iota(dist[:], pattern=[[1, 7], [4, 128]], base=-3, channel_multiplier=-4, allow_small_or_imprecise_dtypes=True)
         make_identity(nc, ident[:])
-        nc.gpsimd.iota(far[:], pattern=[[1, 7], [4, 128]], base=509, channel_multiplier=-4, allow_small_or_imprecise_dtypes=True)
         nc.vector.scalar_tensor_tensor(out=near[:], in0=dist[:], scalar=-BIG, in1=dist[:], op0=ALU.mult, op1=ALU.max)
         nc.vector.tensor_scalar(out=nd[:], in0=dk[:].rearrange("p g t -> p (g t)"), scalar1=1.0 / 2.0**90, scalar2=-1.0, op0=ALU.max, op1=ALU.mult)
+        nc.vector.tensor_scalar(out=far_bias[:], in0=nd[:, 0:4], scalar1=512.0, scalar2=LOG_SCALE, op0=ALU.mult, op1=ALU.add)
 
         DUMMY(6)
         EX(0, 0)

@@ -13,340 +13,326 @@ FP8X4 = mybir.dt.float8_e4m3fn_x4
 ALU = mybir.AluOpType
 ACT = mybir.ActivationFunctionType
 
-FLOPS = 2 * 1024 * (512 * 512 + 512 * 1024) * 2
-BIG = 2.0**100
+P = 128
+CHUNK = 512
+CHUNKS = 2
+BLOCKS = 4
+FEATURES = 1024
+HALF = 512
+
+FLOPS = 2 * FEATURES * (CHUNK * CHUNK + CHUNK * 2 * CHUNK) * 2
+
+FAR = 2.0**100
+MIN_DECAY = 2.0**-90
 LOG_SCALE = -5.0 * math.log(2.0)
 
 
 def tile_simplifiedretnet_pa_kernel(tc, q, k, v_bytes, v_scale, decay, out):
     nc = tc.nc
-    x_rows = {
-        "q": q.rearrange("o (c m b) f -> (o c) m b f", c=2, b=4),
-        "k": k.rearrange("o (c m b) f -> (o c) m b f", c=2, b=4),
+    rows = {
+        "q": q.rearrange("o (c m b) f -> (o c) m b f", c=CHUNKS, b=BLOCKS),
+        "k": k.rearrange("o (c m b) f -> (o c) m b f", c=CHUNKS, b=BLOCKS),
+        "v": v_bytes.rearrange("o (c m b) n -> (o c) m b n", c=CHUNKS, b=BLOCKS),
     }
-    v_rows = v_bytes.rearrange("o (g p t) n -> (o g) p t n", g=2, t=4)
-    o_rows = out.rearrange("o (c m b) n -> (o c) m b n", c=2, b=4)
+    out_rows = out.rearrange("o (c m b) n -> (o c) m b n", c=CHUNKS, b=BLOCKS)
 
     with ExitStack() as ctx:
         keep = ctx.enter_context(tc.tile_pool(name="keep", bufs=1))
-        ps_tp = ctx.enter_context(tc.psum_pool(name="ps_tp", bufs=3))
-        ps_sc = ctx.enter_context(tc.psum_pool(name="ps_sc", bufs=2))
-        ps_po = ctx.enter_context(tc.psum_pool(name="ps_po", bufs=3))
+        turned_banks = ctx.enter_context(tc.psum_pool(name="turned_banks", bufs=3))
+        score_banks = ctx.enter_context(tc.psum_pool(name="score_banks", bufs=2))
+        sum_banks = ctx.enter_context(tc.psum_pool(name="sum_banks", bufs=3))
         ctx.enter_context(tc.manual_schedule())
 
         def sb(name, shape, dtype):
             return keep.tile(shape, dtype, name=name, align_bytes=64)
 
-        raw = {(x, c): sb("raw_%s_%s" % (x, c,), [128, 4, 1024], BF16) for x in "qk" for c in range(2)}
-        grouped = {(x, c, b): sb("grp_%s_%s_%s" % (x, c, b,), [128, 2, 128, 2], F32) for x in "qk" for c in range(2) for b in range(4)}
-        codes = {(x, c, b): sb("cod_%s_%s_%s" % (x, c, b,), [128, 256], U32) for x in "qk" for c in range(2) for b in range(4)}
-        scales = {(x, c, b): sb("scl_%s_%s_%s" % (x, c, b,), [128, 256], U8) for x in "qk" for c in range(2) for b in range(4)}
-        vb = [sb("vb%s" % (g,), [128, 4, 1024], U8) for g in range(2)]
-        wide = [sb("wide%s" % (g,), [128, 4, 1024], BF16) for g in range(2)]
-        vi = {(g, h): sb("vi%s_%s" % (g, h,), [128, 512, 4], BF16) for g in range(2) for h in range(2)}
-        v_codes = {(g, h): sb("vc%s_%s" % (g, h,), [128, 512], U32) for g in range(2) for h in range(2)}
-        v_scl = {(g, h): sb("vx%s_%s" % (g, h,), [128, 512], U8) for g in range(2) for h in range(2)}
-        gain = [sb("gain%s" % (e,), [128, 128, 16], F32) for e in range(3)]
-        pairs = [(0, 0), (0, 1), (1, 1)]
-        s_bf = {(g, c, b): sb("s%s_%s_%s" % (g, c, b,), [128, 128, 4], BF16) for g, c in pairs for b in range(4)}
-        s_codes = {(g, c, b): sb("sc%s_%s_%s" % (g, c, b,), [128, 128], U32) for g, c in pairs for b in range(4)}
-        s_scl = {(g, c, b): sb("sx%s_%s_%s" % (g, c, b,), [128, 128], U8) for g, c in pairs for b in range(4)}
-        result = {(c, b, h): sb("o%s_%s_%s" % (c, b, h,), [128, 512], F32) for c in range(2) for b in range(4) for h in range(2)}
-        ident = sb("ident", [128, 128], F32)
-        dist = sb("dist", [128, 7, 128], F32)
-        near = sb("near", [128, 7, 128], F32)
-        far_bias = sb("far_bias", [128, 4], F32)
-        dk = sb("dk", [128, 2, 4], BF16)
-        nd = sb("nd", [128, 8], F32)
-        vs = sb("vs", [128, 2, 4], F32)
-        warm = sb("warm", [128, 8], F32)
-        warm_out = sb("warm_out", [128, 8], F32)
-        zeros = sb("zeros", [128, 512], BF16)
+        chunks = range(CHUNKS)
+        pairs = range(BLOCKS // 2)
+        halves = range(FEATURES // HALF)
+        squares = [(0, 0), (0, 1), (1, 1)]
+        x_chunks = [(x, c) for x in "qk" for c in chunks]
+        raw = {(x, c): sb("raw_%s%d" % (x, c), [P, BLOCKS, FEATURES], BF16) for x, c in x_chunks}
+        x_words = {(x, c, j): sb("words_%s%d%d" % (x, c, j), [P, 2, 2, P, 2], F32) for x, c in x_chunks for j in pairs}
+        x_codes = {(x, c, j): sb("codes_%s%d%d" % (x, c, j), [P, 2 * 2 * P], U32) for x, c in x_chunks for j in pairs}
+        x_scales = {(x, c, j): sb("scales_%s%d%d" % (x, c, j), [P, 2 * 2 * P], U8) for x, c in x_chunks for j in pairs}
+        v_raw = [sb("v_raw%d" % g, [P, BLOCKS, FEATURES], U8) for g in chunks]
+        v_wide = [sb("v_wide%d" % g, [P, BLOCKS, FEATURES], BF16) for g in chunks]
+        v_words = {(g, h): sb("v_words%d%d" % (g, h), [P, HALF, BLOCKS], BF16) for g in chunks for h in halves}
+        v_codes = {(g, h): sb("v_codes%d%d" % (g, h), [P, HALF], U32) for g in chunks for h in halves}
+        v_scales = {(g, h): sb("v_scales%d%d" % (g, h), [P, HALF], U8) for g in chunks for h in halves}
+        gains = {(g, c): sb("gains%d%d" % (g, c), [P, P, 4 * BLOCKS], F32) for g, c in squares}
+        s_words = {(g, c, j): sb("s_words%d%d%d" % (g, c, j), [P, 2, P, BLOCKS], BF16) for g, c in squares for j in pairs}
+        s_codes = {(g, c, j): sb("s_codes%d%d%d" % (g, c, j), [P, 2 * P], U32) for g, c in squares for j in pairs}
+        s_scales = {(g, c, j): sb("s_scales%d%d%d" % (g, c, j), [P, 2 * P], U8) for g, c in squares for j in pairs}
+        result = {(c, b): sb("result%d%d" % (c, b), [P, FEATURES], F32) for c in chunks for b in range(BLOCKS)}
+        ident = sb("ident", [P, P], F32)
+        distance = sb("distance", [P, 2 * BLOCKS - 1, P], F32)
+        masked_distance = sb("masked_distance", [P, 2 * BLOCKS - 1, P], F32)
+        decay_in = sb("decay_in", [P, CHUNKS, BLOCKS], BF16)
+        minus_decay = sb("minus_decay", [P, CHUNKS * BLOCKS], F32)
+        far_bias = sb("far_bias", [P, BLOCKS], F32)
+        v_scale_in = sb("v_scale_in", [P, CHUNKS, BLOCKS], F32)
+        table_in = sb("table_in", [P, 8], F32)
+        table_out = sb("table_out", [P, 8], F32)
 
-        psum = {}
+        bank = {}
 
-        def load(name, c, lo, hi):
-            if name == "v":
-                nc.sync.dma_start(out=vb[c][:, lo:hi, :], in_=v_rows[c][:, lo:hi, :])
-            else:
-                nc.sync.dma_start(out=raw[name, c][:, lo:hi, :], in_=x_rows[name][c][:, lo:hi, :])
+        def load(x, c, first):
+            tile = v_raw[c] if x == "v" else raw[x, c]
+            nc.sync.dma_start(out=tile[:, first : first + 2, :], in_=rows[x][c][:, first : first + 2, :])
 
-        def TR(x, c, b):
-            bank = ps_tp.tile([128, 2, 2, 128], F32, name="tp")
-            psum[x, c, b] = bank
+        def turn(x, c, b, on_vector=False):
+            bank[x, c, b] = turned_banks.tile([P, 2, 2, P], F32, name="turned")
             words = raw[x, c][:, b, :].bitcast(F32)
-            for g in range(2):
+            for f in range(2):
                 for u in range(2):
-                    nc.tensor.transpose(bank[:, g, u, :], words[:, 256 * g + u : 256 * (g + 1) : 2], ident[:])
-
-        def CP(x, c, b, eng="S"):
-            src = psum[x, c, b][:].rearrange("p g u r -> p g r u")
-            if eng == "S":
-                nc.scalar.copy(grouped[x, c, b][:], src)
+                    nc.tensor.transpose(bank[x, c, b][:, f, u, :], words[:, 256 * f + u : 256 * (f + 1) : 2], ident[:])
+            to = x_words[x, c, b // 2][:, b % 2]
+            by_row = bank[x, c, b][:].rearrange("p f u r -> p f r u")
+            if on_vector:
+                nc.vector.tensor_copy(out=to, in_=by_row)
             else:
-                nc.vector.tensor_copy(out=grouped[x, c, b][:], in_=src)
+                nc.scalar.copy(to, by_row)
 
-        def QZ(x, c, b):
+        def quantize_x(x, c, j):
             nc.vector.quantize_mx(
-                out=codes[x, c, b][:].bitcast(FP8X4),
-                scales=scales[x, c, b][:],
-                in_=grouped[x, c, b][:].rearrange("p g r u -> p (g r u)").bitcast(BF16),
+                out=x_codes[x, c, j][:].bitcast(FP8X4),
+                scales=x_scales[x, c, j][:],
+                in_=x_words[x, c, j][:].rearrange("p b f r u -> p (b f r u)").bitcast(BF16),
             )
 
-        def WD(g, t, eng="V"):
-            src = vb[g][:, t, :].bitcast(E4M3FN)
-            if eng == "V":
-                nc.vector.tensor_scalar(out=wide[g][:, t, :], in0=src, scalar1=vs[:, g, t : t + 1], scalar2=None, op0=ALU.mult)
-            else:
-                nc.scalar.activation(out=wide[g][:, t, :], in_=src, func=ACT.Copy, scale=vs[:, g, t : t + 1])
+        def widen(g):
+            for t in range(BLOCKS):
+                widen_block(g, t)
 
-        def IL(g, h):
+        def widen_block(g, t):
+            codes = v_raw[g][:, t, :].bitcast(E4M3FN)
+            scale = v_scale_in[:, g, t : t + 1]
+            if t < BLOCKS - 1:
+                nc.vector.tensor_scalar(out=v_wide[g][:, t, :], in0=codes, scalar1=scale, scalar2=None, op0=ALU.mult)
+            else:
+                nc.scalar.activation(out=v_wide[g][:, t, :], in_=codes, func=ACT.Copy, scale=scale)
+
+        def interleave_v(g, h):
             nc.vector.tensor_copy(
-                out=vi[g, h][:].rearrange("p (m i) t -> p m t i", i=4),
-                in_=wide[g][:, :, 512 * h : 512 * (h + 1)].rearrange("p t (m i) -> p m t i", i=4),
+                out=v_words[g, h][:].rearrange("p (n i) t -> p n t i", i=4),
+                in_=v_wide[g][:, :, HALF * h : HALF * (h + 1)].rearrange("p t (n i) -> p n t i", i=4),
             )
 
-        def QV(g, h):
+        def quantize_v(g, h):
             nc.vector.quantize_mx(
-                out=v_codes[g, h][:].bitcast(FP8X4), scales=v_scl[g, h][:], in_=vi[g, h][:].rearrange("p n t -> p (n t)")
+                out=v_codes[g, h][:].bitcast(FP8X4),
+                scales=v_scales[g, h][:],
+                in_=v_words[g, h][:].rearrange("p n t -> p (n t)"),
             )
 
-        def EX(e, t):
-            table = dist if e == 1 else near
-            col = 4 * (e // 2) + t
-            nc.scalar.activation(
-                out=gain[e][:, :, 4 * t : 4 * (t + 1)],
-                in_=table[:, 3 - t : 7 - t, :].rearrange("p b (m i) -> p (b m) i", i=4),
-                func=ACT.Exp,
-                bias=far_bias[:, t : t + 1] if e == 1 else LOG_SCALE,
-                scale=nd[:, col : col + 1],
-            )
+        def gain(g, c, *ts):
+            for t in ts:
+                table = masked_distance if g == c else distance
+                column = BLOCKS * g + t
+                nc.scalar.activation(
+                    out=gains[g, c][:, :, 4 * t : 4 * (t + 1)],
+                    in_=table[:, 3 - t : 7 - t, :].rearrange("p b (m i) -> p (b m) i", i=4),
+                    func=ACT.Exp,
+                    bias=LOG_SCALE if g == c else far_bias[:, t : t + 1],
+                    scale=minus_decay[:, column : column + 1],
+                )
 
-        def M1(g, c, b, pool="sc"):
-            bank = (ps_sc if pool == "sc" else ps_tp).tile([128, 4, 128], F32, name=pool)
-            psum["s", g, c, b] = bank
-            for t in range(4):
+        def score(g, c, b, pool=score_banks):
+            name = "scores" if pool is score_banks else "turned"
+            bank[g, c, b] = pool.tile([P, BLOCKS, P], F32, name=name)
+            for t in range(BLOCKS):
                 for f in range(2):
-                    cols = slice(128 * f, 128 * (f + 1))
+                    k_cols = slice(P * (2 * (t % 2) + f), P * (2 * (t % 2) + f + 1))
+                    q_cols = slice(P * (2 * (b % 2) + f), P * (2 * (b % 2) + f + 1))
                     nc.tensor.matmul_mx(
-                        out=bank[:, t, :],
-                        lhsT=codes["k", g, t][:, cols].bitcast(FP8X4),
-                        lhsT_scale=scales["k", g, t][:, cols],
-                        rhs=codes["q", c, b][:, cols].bitcast(FP8X4),
-                        rhs_scale=scales["q", c, b][:, cols],
+                        out=bank[g, c, b][:, t, :],
+                        lhsT=x_codes["k", g, t // 2][:, k_cols].bitcast(FP8X4),
+                        lhsT_scale=x_scales["k", g, t // 2][:, k_cols],
+                        rhs=x_codes["q", c, b // 2][:, q_cols].bitcast(FP8X4),
+                        rhs_scale=x_scales["q", c, b // 2][:, q_cols],
                         start=(f == 0),
                         stop=(f == 1),
                     )
 
-        def MK(g, c, b):
-            nc.vector.tensor_tensor(
-                out=s_bf[g, c, b][:].rearrange("p (m i) t -> p m t i", i=4),
-                in0=psum["s", g, c, b][:].rearrange("p t (m i) -> p m t i", i=4),
-                in1=gain[g + c][:, 32 * b : 32 * (b + 1), :].rearrange("p m (t i) -> p m t i", i=4),
-                op=ALU.mult,
-            )
+        def weigh(g, c, *bs):
+            for b in bs:
+                nc.vector.tensor_tensor(
+                    out=s_words[g, c, b // 2][:, b % 2].rearrange("p (m i) t -> p m t i", i=4),
+                    in0=bank[g, c, b][:].rearrange("p t (m i) -> p m t i", i=4),
+                    in1=gains[g, c][:, 32 * b : 32 * (b + 1), :].rearrange("p m (t i) -> p m t i", i=4),
+                    op=ALU.mult,
+                )
 
-        def QS(g, c, b):
+        def quantize_s(g, c, *bs):
+            j, first, width = bs[0] // 2, P * (bs[0] % 2), P * len(bs)
             nc.vector.quantize_mx(
-                out=s_codes[g, c, b][:].bitcast(FP8X4),
-                scales=s_scl[g, c, b][:],
-                in_=s_bf[g, c, b][:].rearrange("p i t -> p (i t)"),
+                out=s_codes[g, c, j][:, first : first + width].bitcast(FP8X4),
+                scales=s_scales[g, c, j][:, first : first + width],
+                in_=s_words[g, c, j][:].rearrange("p b i t -> p (b i t)")[:, 4 * first : 4 * (first + width)],
             )
 
-        def M2(c, b, h, gs=None, pool="po"):
-            if gs is None:
-                gs = range(c + 1)
-            if ("o", c, b, h) not in psum:
-                psum["o", c, b, h] = (ps_po if pool == "po" else ps_tp).tile([128, 512], F32, name=pool)
+        def multiply_v(c, b, h, gs):
+            if gs[0] == 0:
+                bank["out", c, b, h] = sum_banks.tile([P, HALF], F32, name="sums")
+            s_cols = slice(P * (b % 2), P * (b % 2 + 1))
             for g in gs:
                 nc.tensor.matmul_mx(
-                    out=psum["o", c, b, h][:],
-                    lhsT=s_codes[g, c, b][:].bitcast(FP8X4),
-                    lhsT_scale=s_scl[g, c, b][:],
+                    out=bank["out", c, b, h][:],
+                    lhsT=s_codes[g, c, b // 2][:, s_cols].bitcast(FP8X4),
+                    lhsT_scale=s_scales[g, c, b // 2][:, s_cols],
                     rhs=v_codes[g, h][:].bitcast(FP8X4),
-                    rhs_scale=v_scl[g, h][:],
+                    rhs_scale=v_scales[g, h][:],
                     start=(g == 0),
                     stop=(g == c),
                 )
 
-        def CO(c, b, h, eng="S"):
-            src = psum["o", c, b, h]
-            res = result[c, b, h]
-            if eng == "S":
-                nc.scalar.copy(res[:], src[:])
+        def copy_out(c, b, h, on_vector=False):
+            to = result[c, b][:, HALF * h : HALF * (h + 1)]
+            if on_vector:
+                nc.vector.tensor_copy(out=to, in_=bank["out", c, b, h][:])
             else:
-                nc.vector.tensor_copy(out=res[:], in_=src[:])
-            nc.sync.dma_start(out=o_rows[c][:, b, 512 * h : 512 * (h + 1)], in_=res[:])
+                nc.scalar.copy(to, bank["out", c, b, h][:])
 
-        def DUMMY(n, width=512):
-            bank = ps_sc.tile([128, 512], F32, name="sc")
-            for i in range(n):
-                nc.tensor.matmul(bank[:, :width], lhsT=zeros[:, :128], rhs=zeros[:, :width], start=True, stop=True)
+        def store(c, b, first=0, last=FEATURES):
+            nc.sync.dma_start(out=out_rows[c][:, b, first:last], in_=result[c, b][:, first:last])
 
-        nc.scalar.dma_start(out=dk[:], in_=decay.rearrange("(g p t) -> p g t", g=2, t=4))
-        nc.scalar.dma_start(out=vs[:], in_=v_scale.rearrange("o (g p t) i -> p (o g) (t i)", g=2, t=4))
-        load("v", 0, 0, 2)
-        load("v", 0, 2, 4)
-        for x, c in (("k", 0), ("q", 0), ("q", 1), ("k", 1)):
-            load(x, c, 0, 2)
-            load(x, c, 2, 4)
-        load("v", 1, 0, 4)
-        nc.vector.memset(warm[:], 0.0)
-        nc.vector.memset(zeros[:], 0.0)
-        nc.scalar.activation(out=warm_out[:], in_=warm[:], func=ACT.Exp)
-        nc.gpsimd.iota(dist[:], pattern=[[1, 7], [4, 128]], base=-3, channel_multiplier=-4, allow_small_or_imprecise_dtypes=True)
+        def finish(c, b):
+            copy_out(c, b, 0)
+            copy_out(c, b, 1)
+            store(c, b)
+
+        def finish_by_halves(c, b, vector_half=None):
+            for h in halves:
+                copy_out(c, b, h, h == vector_half)
+                store(c, b, HALF * h, HALF * (h + 1))
+
+        nc.scalar.dma_start(out=decay_in[:], in_=decay.rearrange("(c p t) -> p c t", c=CHUNKS, t=BLOCKS))
+        nc.scalar.dma_start(out=v_scale_in[:], in_=v_scale.rearrange("o (c p t) i -> p (o c) (t i)", c=CHUNKS, t=BLOCKS))
+        load("v", 0, 0)
+        load("k", 0, 0)
+        load("v", 0, 2)
+        load("v", 1, 0)
+        load("k", 0, 2)
+        load("q", 0, 0)
+        load("q", 0, 2)
+        load("q", 1, 0)
+        load("v", 1, 2)
+        load("k", 1, 0)
+        load("k", 1, 2)
+        load("q", 1, 2)
+
+        nc.vector.memset(table_in[:], 0.0)
+        nc.scalar.activation(out=table_out[:], in_=table_in[:], func=ACT.Exp)
+        nc.gpsimd.iota(
+            distance[:], pattern=[[1, 7], [4, P]], base=-3, channel_multiplier=-4, allow_small_or_imprecise_dtypes=True
+        )
         make_identity(nc, ident[:])
-        nc.vector.scalar_tensor_tensor(out=near[:], in0=dist[:], scalar=-BIG, in1=dist[:], op0=ALU.mult, op1=ALU.max)
-        nc.vector.tensor_scalar(out=nd[:], in0=dk[:].rearrange("p g t -> p (g t)"), scalar1=1.0 / 2.0**90, scalar2=-1.0, op0=ALU.max, op1=ALU.mult)
-        nc.vector.tensor_scalar(out=far_bias[:], in0=nd[:, 0:4], scalar1=512.0, scalar2=LOG_SCALE, op0=ALU.mult, op1=ALU.add)
+        nc.vector.scalar_tensor_tensor(
+            out=masked_distance[:], in0=distance[:], scalar=-FAR, in1=distance[:], op0=ALU.mult, op1=ALU.max
+        )
+        nc.vector.tensor_scalar(
+            out=minus_decay[:],
+            in0=decay_in[:].rearrange("p c t -> p (c t)"),
+            scalar1=MIN_DECAY,
+            scalar2=-1.0,
+            op0=ALU.max,
+            op1=ALU.mult,
+        )
+        nc.vector.tensor_scalar(
+            out=far_bias[:], in0=minus_decay[:, 0:BLOCKS], scalar1=512.0, scalar2=LOG_SCALE, op0=ALU.mult, op1=ALU.add
+        )
 
-        DUMMY(6)
-        EX(0, 0)
-        EX(0, 1)
-        EX(0, 2)
-        EX(0, 3)
-        WD(0, 0, 'V')
-        WD(0, 1, 'V')
-        WD(0, 2, 'V')
-        WD(0, 3, 'V')
-        TR('k', 0, 0)
-        CP('k', 0, 0)
-        TR('k', 0, 1)
-        CP('k', 0, 1)
-        DUMMY(1)
-        TR('k', 0, 2)
-        CP('k', 0, 2)
-        TR('k', 0, 3)
-        CP('k', 0, 3)
-        DUMMY(1)
-        IL(0, 0)
-        QZ('k', 0, 0)
-        QZ('k', 0, 1)
-        QZ('k', 0, 2)
-        QZ('k', 0, 3)
-        TR('q', 0, 0)
-        CP('q', 0, 0)
-        TR('q', 0, 1)
-        CP('q', 0, 1)
-        DUMMY(1)
-        TR('q', 0, 2)
-        CP('q', 0, 2)
-        TR('q', 0, 3)
-        CP('q', 0, 3)
-        QZ('q', 0, 0)
-        QZ('q', 0, 1)
-        M1(0, 0, 0)
-        M1(0, 0, 1)
-        IL(0, 1)
-        EX(1, 0)
-        EX(1, 1)
-        TR('q', 1, 0)
-        CP('q', 1, 0)
-        TR('q', 1, 1)
-        CP('q', 1, 1)
-        TR('q', 1, 2)
-        CP('q', 1, 2)
-        QZ('q', 0, 2)
-        MK(0, 0, 0)
-        QZ('q', 0, 3)
-        MK(0, 0, 1)
-        QV(0, 0)
-        QS(0, 0, 0)
-        M1(0, 0, 2)
-        M1(0, 0, 3)
-        EX(1, 2)
-        EX(1, 3)
-        TR('q', 1, 3)
-        CP('q', 1, 3)
-        QZ('q', 1, 0)
-        QV(0, 1)
-        MK(0, 0, 2)
-        QS(0, 0, 1)
-        QZ('q', 1, 1)
-        MK(0, 0, 3)
-        QS(0, 0, 2)
-        QZ('q', 1, 2)
-        TR('k', 1, 0)
-        CP('k', 1, 0)
-        TR('k', 1, 1)
-        CP('k', 1, 1)
-        TR('k', 1, 2)
-        CP('k', 1, 2)
-        QZ('q', 1, 3)
-        QS(0, 0, 3)
-        M1(0, 1, 0)
-        M1(0, 1, 1)
-        WD(1, 0, 'V')
-        WD(1, 1, 'V')
-        WD(1, 2, 'V')
-        TR('k', 1, 3)
-        CP('k', 1, 3)
-        M2(0, 0, 0)
-        M2(0, 1, 0)
-        M2(0, 2, 0)
-        WD(1, 3, 'S')
-        QZ('k', 1, 0)
-        MK(0, 1, 0)
-        QZ('k', 1, 1)
-        CO(0, 0, 0)
-        CO(0, 1, 0)
-        CO(0, 2, 0)
-        QZ('k', 1, 2)
-        QS(0, 1, 0)
-        MK(0, 1, 1)
-        QZ('k', 1, 3)
-        M1(0, 1, 2)
-        M1(1, 1, 0, 'tp')
-        M1(1, 1, 1, 'tp')
-        QS(0, 1, 1)
-        IL(1, 0)
-        IL(1, 1)
-        EX(2, 0)
-        EX(2, 1)
-        EX(2, 2)
-        EX(2, 3)
-        M2(0, 3, 0)
-        M2(0, 0, 1)
-        M2(0, 1, 1)
-        CO(0, 3, 0)
-        CO(0, 0, 1)
-        CO(0, 1, 1)
-        M1(0, 1, 3)
-        M1(1, 1, 2, 'tp')
-        M2(0, 2, 1)
-        M2(0, 3, 1)
-        CO(0, 2, 1)
-        CO(0, 3, 1)
-        QV(1, 0)
-        MK(1, 1, 0)
-        QV(1, 1)
-        QS(1, 1, 0)
-        M1(1, 1, 3, 'tp')
-        MK(1, 1, 1)
-        MK(0, 1, 2)
-        M2(1, 0, 0)
-        CO(1, 0, 0)
-        M2(1, 0, 1)
-        CO(1, 0, 1)
-        QS(1, 1, 1)
-        MK(1, 1, 2)
-        QS(0, 1, 2)
-        M2(1, 1, 0)
-        CO(1, 1, 0)
-        M2(1, 1, 1)
-        CO(1, 1, 1)
-        MK(0, 1, 3)
-        QS(1, 1, 2)
-        M2(1, 2, 0)
-        CO(1, 2, 0)
-        M2(1, 2, 1)
-        CO(1, 2, 1)
-        MK(1, 1, 3)
-        QS(0, 1, 3)
-        QS(1, 1, 3)
-        M2(1, 3, 0, (0,))
-        M2(1, 3, 1, (0,))
-        M2(1, 3, 0, (1,))
-        CO(1, 3, 0)
-        M2(1, 3, 1, (1,))
-        CO(1, 3, 1, 'V')
+        gain(0, 0, 0, 1, 2, 3)
+        widen(0)
+        turn("k", 0, 0, on_vector=True)
+        turn("k", 0, 1)
+        widen_block(1, 0)
+        widen_block(1, 1)
+        turn("k", 0, 2)
+        turn("q", 0, 0)
+        turn("k", 0, 3)
+        for b in (1, 2, 3):
+            turn("q", 0, b)
+        interleave_v(0, 0)
+        quantize_x("k", 0, 0)
+        quantize_x("k", 0, 1)
+        quantize_v(0, 0)
+        quantize_x("q", 0, 0)
+        interleave_v(0, 1)
+        gain(0, 1, 0, 1)
+        turn("q", 1, 0)
+        turn("q", 1, 1)
+        quantize_x("q", 0, 1)
+
+        score(0, 0, 0)
+        score(0, 0, 1)
+        gain(0, 1, 2, 3)
+        weigh(0, 0, 0, 1)
+        quantize_x("q", 1, 0)
+        quantize_v(0, 1)
+        widen_block(1, 3)
+        turn("k", 1, 0)
+        score(0, 0, 2)
+        turn("k", 1, 1)
+        score(0, 0, 3)
+        weigh(0, 0, 2)
+        quantize_s(0, 0, 0, 1)
+        widen_block(1, 2)
+        weigh(0, 0, 3)
+        interleave_v(1, 0)
+        gain(1, 1, 0)
+        score(0, 1, 0)
+        multiply_v(0, 0, 0, [0])
+        copy_out(0, 0, 0)
+        for b in (2, 3):
+            turn("q", 1, b)
+            turn("k", 1, b)
+        weigh(0, 1, 0)
+        quantize_s(0, 0, 2, 3)
+        quantize_v(1, 0)
+        quantize_x("q", 1, 1)
+        quantize_x("k", 1, 0)
+        quantize_x("k", 1, 1)
+
+        multiply_v(0, 0, 1, [0])
+        copy_out(0, 0, 1)
+        store(0, 0)
+        score(0, 1, 1)
+        multiply_v(0, 1, 0, [0])
+        multiply_v(0, 1, 1, [0])
+        finish(0, 1)
+        gain(1, 1, 1, 2, 3)
+        score(0, 1, 2, turned_banks)
+        multiply_v(0, 2, 0, [0])
+        multiply_v(0, 2, 1, [0])
+        score(1, 1, 0, turned_banks)
+        multiply_v(0, 3, 0, [0])
+        score(1, 1, 1, turned_banks)
+        finish(0, 2)
+        weigh(0, 1, 1, 2)
+        interleave_v(1, 1)
+        score(0, 1, 3)
+        multiply_v(0, 3, 1, [0])
+        finish(0, 3)
+        score(1, 1, 2)
+        weigh(1, 1, 0, 1)
+        quantize_s(0, 1, 0, 1)
+        quantize_s(1, 1, 0, 1)
+        quantize_v(1, 1)
+        score(1, 1, 3, turned_banks)
+        weigh(0, 1, 3)
+        weigh(1, 1, 2)
+        quantize_s(0, 1, 2, 3)
+        quantize_s(1, 1, 2)
+        weigh(1, 1, 3)
+        quantize_s(1, 1, 3)
+
+        for b in range(3):
+            for h in halves:
+                multiply_v(1, b, h, [0, 1])
+            finish_by_halves(1, b, 1 if b == 2 else None)
+        for g in chunks:
+            for h in halves:
+                multiply_v(1, 3, h, [g])
+        finish_by_halves(1, 3, 0)

import math
from contextlib import ExitStack

import concourse.mybir as mybir
from concourse.masks import make_identity

F32 = mybir.dt.float32
BF16 = mybir.dt.bfloat16
U32 = mybir.dt.uint32
U8 = mybir.dt.uint8
E4M3FN = mybir.dt.float8_e4m3fn
FP8X4 = mybir.dt.float8_e4m3fn_x4
ALU = mybir.AluOpType
ACT = mybir.ActivationFunctionType

P = 128
CHUNK = 512
CHUNKS = 2
BLOCKS = 4
FEATURES = 1024
HALF = 512

FLOPS = 2 * FEATURES * (CHUNK * CHUNK + CHUNK * 2 * CHUNK) * 2

FAR = 2.0**100
MIN_DECAY = 2.0**-90
LOG_SCALE = -5.0 * math.log(2.0)


def tile_simplifiedretnet_pa_kernel(tc, q, k, v_bytes, v_scale, decay, out):
    nc = tc.nc
    rows = {
        "q": q.rearrange("o (c m b) f -> (o c) m b f", c=CHUNKS, b=BLOCKS),
        "k": k.rearrange("o (c m b) f -> (o c) m b f", c=CHUNKS, b=BLOCKS),
        "v": v_bytes.rearrange("o (c m b) n -> (o c) m b n", c=CHUNKS, b=BLOCKS),
    }
    out_rows = out.rearrange("o (c m b) n -> (o c) m b n", c=CHUNKS, b=BLOCKS)

    with ExitStack() as ctx:
        keep = ctx.enter_context(tc.tile_pool(name="keep", bufs=1))
        turned_banks = ctx.enter_context(tc.psum_pool(name="turned_banks", bufs=3))
        score_banks = ctx.enter_context(tc.psum_pool(name="score_banks", bufs=2))
        sum_banks = ctx.enter_context(tc.psum_pool(name="sum_banks", bufs=3))
        ctx.enter_context(tc.manual_schedule())

        def sb(name, shape, dtype):
            return keep.tile(shape, dtype, name=name, align_bytes=64)

        chunks = range(CHUNKS)
        pairs = range(BLOCKS // 2)
        halves = range(FEATURES // HALF)
        squares = [(0, 0), (0, 1), (1, 1)]
        x_chunks = [(x, c) for x in "qk" for c in chunks]
        raw = {(x, c): sb("raw_%s%d" % (x, c), [P, BLOCKS, FEATURES], BF16) for x, c in x_chunks}
        x_words = {(x, c, j): sb("words_%s%d%d" % (x, c, j), [P, 2, 2, P, 2], F32) for x, c in x_chunks for j in pairs}
        x_codes = {(x, c, j): sb("codes_%s%d%d" % (x, c, j), [P, 2 * 2 * P], U32) for x, c in x_chunks for j in pairs}
        x_scales = {(x, c, j): sb("scales_%s%d%d" % (x, c, j), [P, 2 * 2 * P], U8) for x, c in x_chunks for j in pairs}
        v_raw = [sb("v_raw%d" % g, [P, BLOCKS, FEATURES], U8) for g in chunks]
        v_wide = [sb("v_wide%d" % g, [P, BLOCKS, FEATURES], BF16) for g in chunks]
        v_words = {(g, h): sb("v_words%d%d" % (g, h), [P, HALF, BLOCKS], BF16) for g in chunks for h in halves}
        v_codes = {(g, h): sb("v_codes%d%d" % (g, h), [P, HALF], U32) for g in chunks for h in halves}
        v_scales = {(g, h): sb("v_scales%d%d" % (g, h), [P, HALF], U8) for g in chunks for h in halves}
        gains = {(g, c): sb("gains%d%d" % (g, c), [P, P, 4 * BLOCKS], F32) for g, c in squares}
        s_words = {(g, c, j): sb("s_words%d%d%d" % (g, c, j), [P, 2, P, BLOCKS], BF16) for g, c in squares for j in pairs}
        s_codes = {(g, c, j): sb("s_codes%d%d%d" % (g, c, j), [P, 2 * P], U32) for g, c in squares for j in pairs}
        s_scales = {(g, c, j): sb("s_scales%d%d%d" % (g, c, j), [P, 2 * P], U8) for g, c in squares for j in pairs}
        result = {(c, b): sb("result%d%d" % (c, b), [P, FEATURES], F32) for c in chunks for b in range(BLOCKS)}
        ident = sb("ident", [P, P], F32)
        distance = sb("distance", [P, 2 * BLOCKS - 1, P], F32)
        masked_distance = sb("masked_distance", [P, 2 * BLOCKS - 1, P], F32)
        decay_in = sb("decay_in", [P, CHUNKS, BLOCKS], BF16)
        minus_decay = sb("minus_decay", [P, CHUNKS * BLOCKS], F32)
        far_bias = sb("far_bias", [P, BLOCKS], F32)
        v_scale_in = sb("v_scale_in", [P, CHUNKS, BLOCKS], F32)
        table_in = sb("table_in", [P, 8], F32)
        table_out = sb("table_out", [P, 8], F32)

        bank = {}

        def load(x, c, first):
            tile = v_raw[c] if x == "v" else raw[x, c]
            nc.sync.dma_start(out=tile[:, first : first + 2, :], in_=rows[x][c][:, first : first + 2, :])

        def turn(x, c, b, on_vector=False):
            bank[x, c, b] = turned_banks.tile([P, 2, 2, P], F32, name="turned")
            words = raw[x, c][:, b, :].bitcast(F32)
            for f in range(2):
                for u in range(2):
                    nc.tensor.transpose(bank[x, c, b][:, f, u, :], words[:, 256 * f + u : 256 * (f + 1) : 2], ident[:])
            to = x_words[x, c, b // 2][:, b % 2]
            by_row = bank[x, c, b][:].rearrange("p f u r -> p f r u")
            if on_vector:
                nc.vector.tensor_copy(out=to, in_=by_row)
            else:
                nc.scalar.copy(to, by_row)

        def quantize_x(x, c, j):
            nc.vector.quantize_mx(
                out=x_codes[x, c, j][:].bitcast(FP8X4),
                scales=x_scales[x, c, j][:],
                in_=x_words[x, c, j][:].rearrange("p b f r u -> p (b f r u)").bitcast(BF16),
            )

        def widen(g):
            for t in range(BLOCKS):
                widen_block(g, t)

        def widen_block(g, t):
            codes = v_raw[g][:, t, :].bitcast(E4M3FN)
            scale = v_scale_in[:, g, t : t + 1]
            if t < BLOCKS - 1:
                nc.vector.tensor_scalar(out=v_wide[g][:, t, :], in0=codes, scalar1=scale, scalar2=None, op0=ALU.mult)
            else:
                nc.scalar.activation(out=v_wide[g][:, t, :], in_=codes, func=ACT.Copy, scale=scale)

        def interleave_v(g, h):
            nc.vector.tensor_copy(
                out=v_words[g, h][:].rearrange("p (n i) t -> p n t i", i=4),
                in_=v_wide[g][:, :, HALF * h : HALF * (h + 1)].rearrange("p t (n i) -> p n t i", i=4),
            )

        def quantize_v(g, h):
            nc.vector.quantize_mx(
                out=v_codes[g, h][:].bitcast(FP8X4),
                scales=v_scales[g, h][:],
                in_=v_words[g, h][:].rearrange("p n t -> p (n t)"),
            )

        def gain(g, c, *ts):
            for t in ts:
                table = masked_distance if g == c else distance
                column = BLOCKS * g + t
                nc.scalar.activation(
                    out=gains[g, c][:, :, 4 * t : 4 * (t + 1)],
                    in_=table[:, 3 - t : 7 - t, :].rearrange("p b (m i) -> p (b m) i", i=4),
                    func=ACT.Exp,
                    bias=LOG_SCALE if g == c else far_bias[:, t : t + 1],
                    scale=minus_decay[:, column : column + 1],
                )

        def score(g, c, b, pool=score_banks):
            name = "scores" if pool is score_banks else "turned"
            bank[g, c, b] = pool.tile([P, BLOCKS, P], F32, name=name)
            for t in range(BLOCKS):
                for f in range(2):
                    k_cols = slice(P * (2 * (t % 2) + f), P * (2 * (t % 2) + f + 1))
                    q_cols = slice(P * (2 * (b % 2) + f), P * (2 * (b % 2) + f + 1))
                    nc.tensor.matmul_mx(
                        out=bank[g, c, b][:, t, :],
                        lhsT=x_codes["k", g, t // 2][:, k_cols].bitcast(FP8X4),
                        lhsT_scale=x_scales["k", g, t // 2][:, k_cols],
                        rhs=x_codes["q", c, b // 2][:, q_cols].bitcast(FP8X4),
                        rhs_scale=x_scales["q", c, b // 2][:, q_cols],
                        start=(f == 0),
                        stop=(f == 1),
                    )

        def weigh(g, c, *bs):
            for b in bs:
                nc.vector.tensor_tensor(
                    out=s_words[g, c, b // 2][:, b % 2].rearrange("p (m i) t -> p m t i", i=4),
                    in0=bank[g, c, b][:].rearrange("p t (m i) -> p m t i", i=4),
                    in1=gains[g, c][:, 32 * b : 32 * (b + 1), :].rearrange("p m (t i) -> p m t i", i=4),
                    op=ALU.mult,
                )

        def quantize_s(g, c, *bs):
            j, first, width = bs[0] // 2, P * (bs[0] % 2), P * len(bs)
            nc.vector.quantize_mx(
                out=s_codes[g, c, j][:, first : first + width].bitcast(FP8X4),
                scales=s_scales[g, c, j][:, first : first + width],
                in_=s_words[g, c, j][:].rearrange("p b i t -> p (b i t)")[:, 4 * first : 4 * (first + width)],
            )

        def multiply_v(c, b, h, gs):
            if gs[0] == 0:
                bank["out", c, b, h] = sum_banks.tile([P, HALF], F32, name="sums")
            s_cols = slice(P * (b % 2), P * (b % 2 + 1))
            for g in gs:
                nc.tensor.matmul_mx(
                    out=bank["out", c, b, h][:],
                    lhsT=s_codes[g, c, b // 2][:, s_cols].bitcast(FP8X4),
                    lhsT_scale=s_scales[g, c, b // 2][:, s_cols],
                    rhs=v_codes[g, h][:].bitcast(FP8X4),
                    rhs_scale=v_scales[g, h][:],
                    start=(g == 0),
                    stop=(g == c),
                )

        def copy_out(c, b, h, on_vector=False):
            to = result[c, b][:, HALF * h : HALF * (h + 1)]
            if on_vector:
                nc.vector.tensor_copy(out=to, in_=bank["out", c, b, h][:])
            else:
                nc.scalar.copy(to, bank["out", c, b, h][:])

        def store(c, b, first=0, last=FEATURES):
            nc.sync.dma_start(out=out_rows[c][:, b, first:last], in_=result[c, b][:, first:last])

        def finish(c, b):
            copy_out(c, b, 0)
            copy_out(c, b, 1)
            store(c, b)

        def finish_by_halves(c, b, vector_half=None):
            for h in halves:
                copy_out(c, b, h, h == vector_half)
                store(c, b, HALF * h, HALF * (h + 1))

        nc.scalar.dma_start(out=decay_in[:], in_=decay.rearrange("(c p t) -> p c t", c=CHUNKS, t=BLOCKS))
        nc.scalar.dma_start(out=v_scale_in[:], in_=v_scale.rearrange("o (c p t) i -> p (o c) (t i)", c=CHUNKS, t=BLOCKS))
        load("v", 0, 0)
        load("k", 0, 0)
        load("v", 0, 2)
        load("v", 1, 0)
        load("k", 0, 2)
        load("q", 0, 0)
        load("q", 0, 2)
        load("q", 1, 0)
        load("v", 1, 2)
        load("k", 1, 0)
        load("k", 1, 2)
        load("q", 1, 2)

        nc.vector.memset(table_in[:], 0.0)
        nc.scalar.activation(out=table_out[:], in_=table_in[:], func=ACT.Exp)
        nc.gpsimd.iota(
            distance[:], pattern=[[1, 7], [4, P]], base=-3, channel_multiplier=-4, allow_small_or_imprecise_dtypes=True
        )
        make_identity(nc, ident[:])
        nc.vector.scalar_tensor_tensor(
            out=masked_distance[:], in0=distance[:], scalar=-FAR, in1=distance[:], op0=ALU.mult, op1=ALU.max
        )
        nc.vector.tensor_scalar(
            out=minus_decay[:],
            in0=decay_in[:].rearrange("p c t -> p (c t)"),
            scalar1=MIN_DECAY,
            scalar2=-1.0,
            op0=ALU.max,
            op1=ALU.mult,
        )
        nc.vector.tensor_scalar(
            out=far_bias[:], in0=minus_decay[:, 0:BLOCKS], scalar1=512.0, scalar2=LOG_SCALE, op0=ALU.mult, op1=ALU.add
        )

        gain(0, 0, 0, 1, 2, 3)
        widen(0)
        turn("k", 0, 0, on_vector=True)
        turn("k", 0, 1)
        widen_block(1, 0)
        widen_block(1, 1)
        turn("k", 0, 2)
        turn("q", 0, 0)
        turn("k", 0, 3)
        for b in (1, 2, 3):
            turn("q", 0, b)
        interleave_v(0, 0)
        quantize_x("k", 0, 0)
        quantize_x("k", 0, 1)
        quantize_v(0, 0)
        quantize_x("q", 0, 0)
        interleave_v(0, 1)
        gain(0, 1, 0, 1)
        turn("q", 1, 0)
        turn("q", 1, 1)
        quantize_x("q", 0, 1)

        score(0, 0, 0)
        score(0, 0, 1)
        gain(0, 1, 2, 3)
        weigh(0, 0, 0, 1)
        quantize_x("q", 1, 0)
        quantize_v(0, 1)
        widen_block(1, 3)
        turn("k", 1, 0)
        score(0, 0, 2)
        turn("k", 1, 1)
        score(0, 0, 3)
        weigh(0, 0, 2)
        quantize_s(0, 0, 0, 1)
        widen_block(1, 2)
        weigh(0, 0, 3)
        interleave_v(1, 0)
        gain(1, 1, 0)
        score(0, 1, 0)
        multiply_v(0, 0, 0, [0])
        copy_out(0, 0, 0)
        for b in (2, 3):
            turn("q", 1, b)
            turn("k", 1, b)
        weigh(0, 1, 0)
        quantize_s(0, 0, 2, 3)
        quantize_v(1, 0)
        quantize_x("q", 1, 1)
        quantize_x("k", 1, 0)
        quantize_x("k", 1, 1)

        multiply_v(0, 0, 1, [0])
        copy_out(0, 0, 1)
        store(0, 0)
        score(0, 1, 1)
        multiply_v(0, 1, 0, [0])
        multiply_v(0, 1, 1, [0])
        finish(0, 1)
        gain(1, 1, 1, 2, 3)
        score(0, 1, 2, turned_banks)
        multiply_v(0, 2, 0, [0])
        multiply_v(0, 2, 1, [0])
        score(1, 1, 0, turned_banks)
        multiply_v(0, 3, 0, [0])
        score(1, 1, 1, turned_banks)
        finish(0, 2)
        weigh(0, 1, 1, 2)
        interleave_v(1, 1)
        score(0, 1, 3)
        multiply_v(0, 3, 1, [0])
        finish(0, 3)
        score(1, 1, 2)
        weigh(1, 1, 0, 1)
        quantize_s(0, 1, 0, 1)
        quantize_s(1, 1, 0, 1)
        quantize_v(1, 1)
        score(1, 1, 3, turned_banks)
        weigh(0, 1, 3)
        weigh(1, 1, 2)
        quantize_s(0, 1, 2, 3)
        quantize_s(1, 1, 2)
        weigh(1, 1, 3)
        quantize_s(1, 1, 3)

        for b in range(3):
            for h in halves:
                multiply_v(1, b, h, [0, 1])
            finish_by_halves(1, b, 1 if b == 2 else None)
        for g in chunks:
            for h in halves:
                multiply_v(1, 3, h, [g])
        finish_by_halves(1, 3, 0)
